import numpy as np
import ml_dtypes

BF16 = ml_dtypes.bfloat16


def bf(x):
    return np.asarray(x, np.float32).astype(BF16)


def f32(x):
    return np.asarray(x, np.float32)


def f64(x):
    return np.asarray(x).astype(np.float64)


def striped(idx):
    return np.tile(idx.reshape(-1, 16).T, (8, 1))


H, K, Q, S, N = 256, 2, 3, 2048, 1024


def sigmoid(v):
    return 1.0 / (1.0 + np.exp(-v))


def setup_inputs():
    return {
        "base": f32(np.random.standard_normal((H, S))),
        "child_h": bf(np.random.standard_normal((K * H, N))),
        "child_c": f32(np.random.standard_normal((K * H, N))),
        "f_input": f32(np.random.standard_normal((H, N))),
        "iou_input": f32(np.random.standard_normal((Q * H, N))),
        "w_f": bf(0.05 * np.random.standard_normal((H, H))),
        "w_iou": bf(0.05 * np.random.standard_normal((K * H, Q * H))),
        "offs": striped(np.random.permutation(S)[:N]),
    }


def reference(base, child_h, child_c, f_input, iou_input, w_f, w_iou, offs):
    idx = offs[:16].T.reshape(-1)
    hk = f64(child_h)
    hcols = hk.reshape(K, H, N).transpose(1, 0, 2).reshape(H, K * N)
    f = sigmoid((f64(w_f).T @ hcols).reshape(H, K, N) + f64(f_input)[:, None, :])
    c_aggr = (f * f64(child_c).reshape(K, H, N).transpose(1, 0, 2)).sum(axis=1)
    pre = (f64(w_iou).T @ hk + 2.0 * f64(iou_input)).reshape(Q, H, N)
    gi, go, gu = pre[0], pre[1], pre[2]
    cell = sigmoid(gi) * np.tanh(gu) + c_aggr
    out = f64(base).copy()
    out[:, idx] = sigmoid(go) * np.tanh(cell)
    return out

@@ -1,0 +1,108 @@
+import concourse.mybir as mybir
+
+F32 = mybir.dt.float32
+BF16 = mybir.dt.bfloat16
+U16 = mybir.dt.uint16
+ADD = mybir.AluOpType.add
+MULT = mybir.AluOpType.mult
+SIGMOID = mybir.ActivationFunctionType.Sigmoid
+TANH = mybir.ActivationFunctionType.Tanh
+
+P = 128
+FEATURES, CHILDREN, GATES, STORE, NODES = 256, 2, 3, 2048, 1024
+FEATURE_BLOCKS = FEATURES // P
+HIDDEN_BLOCKS = CHILDREN * FEATURES // P
+PIECE = 512
+PIECES = NODES // PIECE
+GATE_I, GATE_O, GATE_U = 0, 1, 2
+
+FLOPS = 2 * NODES * (CHILDREN * FEATURES * FEATURES + CHILDREN * FEATURES * GATES * FEATURES)
+
+
+def tile_generictreelstmcell_kernel(tc, base, child_h, child_c, f_input, iou_input, w_f, w_iou, offs, out):
+    nc = tc.nc
+    hidden_view = child_h.rearrange("(b p) n -> p b n", p=P)
+    cell_view = child_c.rearrange("(k c) n -> c k n", k=CHILDREN)
+    iou_view = iou_input.rearrange("(q c) n -> c q n", q=GATES)
+
+    with (
+        tc.tile_pool(name="held", bufs=1) as held,
+        tc.tile_pool(name="work", bufs=2) as work,
+        tc.psum_pool(name="psum", bufs=8) as psum,
+    ):
+        offsets = held.tile([P, NODES // 16], U16, name="offsets")
+        nc.sync.dma_start(offsets[:], offs)
+        forget_weights = held.tile([P, FEATURES // P, FEATURES], BF16, name="forget_weights")
+        nc.sync.dma_start(forget_weights[:], w_f.rearrange("(b p) c -> p b c", p=P))
+        hidden = [held.tile([P, HIDDEN_BLOCKS, PIECE], BF16, name=f"hidden{j}") for j in range(PIECES)]
+        nc.sync.dma_start(hidden[0][:], hidden_view[:, :, 0:PIECE])
+        gate_weights = held.tile([P, HIDDEN_BLOCKS, GATES * FEATURES], BF16, name="gate_weights")
+        nc.sync.dma_start(gate_weights[:], w_iou.rearrange("(b p) m -> p b m", p=P))
+
+        windows, forget_in, gates_in, cells_in = [], {}, {}, {}
+        for block in range(FEATURE_BLOCKS):
+            rows = slice(block * P, (block + 1) * P)
+            for piece in range(PIECES):
+                cols = slice(piece * PIECE, (piece + 1) * PIECE)
+                step = (block, piece)
+                if block == 0 and piece > 0:
+                    nc.sync.dma_start(hidden[piece][:], hidden_view[:, :, cols])
+                forget_in[step] = held.tile([P, PIECE], F32, name=f"forget_in{block}{piece}")
+                nc.sync.dma_start(forget_in[step][:], f_input[rows, cols])
+                gates_in[step] = held.tile([P, GATES, PIECE], F32, name=f"gates_in{block}{piece}")
+                nc.sync.dma_start(gates_in[step][:], iou_view[rows, :, cols])
+                cells_in[step] = held.tile([P, CHILDREN, PIECE], F32, name=f"cells_in{block}{piece}")
+                nc.sync.dma_start(cells_in[step][:], cell_view[rows, :, cols])
+                if piece == 0:
+                    windows.append(held.tile([P, STORE], F32, name=f"window{block}"))
+                    nc.sync.dma_start(windows[block][:], base[rows, :])
+
+        for block in range(FEATURE_BLOCKS):
+            rows = slice(block * P, (block + 1) * P)
+            for piece in range(PIECES):
+                step = (block, piece)
+
+                forget = work.tile([P, CHILDREN, PIECE], F32, name="forget")
+                for child in range(CHILDREN):
+                    acc = psum.tile([P, PIECE], F32, name="acc")
+                    for b in range(FEATURES // P):
+                        nc.tensor.matmul(
+                            acc[:],
+                            forget_weights[:, b, rows],
+                            hidden[piece][:, child * (FEATURES // P) + b, :],
+                            start=(b == 0),
+                            stop=(b == FEATURES // P - 1),
+                        )
+                    nc.vector.tensor_tensor(forget[:, child, :], acc[:], forget_in[step][:], ADD)
+                nc.scalar.activation(forget[:], forget[:], SIGMOID)
+
+                gates = work.tile([P, GATES, PIECE], F32, name="gates")
+                for gate in range(GATES):
+                    acc = psum.tile([P, PIECE], F32, name="acc")
+                    for b in range(HIDDEN_BLOCKS):
+                        nc.tensor.matmul(
+                            acc[:],
+                            gate_weights[:, b, gate * FEATURES + block * P : gate * FEATURES + (block + 1) * P],
+                            hidden[piece][:, b, :],
+                            start=(b == 0),
+                            stop=(b == HIDDEN_BLOCKS - 1),
+                        )
+                    nc.vector.scalar_tensor_tensor(gates[:, gate, :], gates_in[step][:, gate, :], 2.0, acc[:], MULT, ADD)
+                nc.scalar.activation(gates[:, GATE_I : GATE_O + 1, :], gates[:, GATE_I : GATE_O + 1, :], SIGMOID)
+                nc.scalar.activation(gates[:, GATE_U, :], gates[:, GATE_U, :], TANH)
+
+                kept = work.tile([P, CHILDREN, PIECE], F32, name="kept")
+                nc.vector.tensor_tensor(kept[:], forget[:], cells_in[step][:], MULT)
+                cell = work.tile([P, PIECE], F32, name="cell")
+                nc.vector.tensor_tensor(cell[:], gates[:, GATE_I, :], gates[:, GATE_U, :], MULT)
+                nc.vector.tensor_tensor(cell[:], cell[:], kept[:, 0, :], ADD)
+                nc.vector.tensor_tensor(cell[:], cell[:], kept[:, 1, :], ADD)
+                nc.scalar.activation(cell[:], cell[:], TANH)
+
+                nc.vector.tensor_tensor(
+                    windows[block][:].indirect(offsets[:, piece * (PIECE // 16) : (piece + 1) * (PIECE // 16)]),
+                    gates[:, GATE_O, :],
+                    cell[:],
+                    MULT,
+                )
+            nc.sync.dma_start(out[rows, :], windows[block][:])

@@ -25,59 +25,71 @@ def tile_generictreelstmcell_kernel(tc, base, child_h, child_c, f_input, iou_inp
     cell_view = child_c.rearrange("(k c) n -> c k n", k=CHILDREN)
     iou_view = iou_input.rearrange("(q c) n -> c q n", q=GATES)
 
+    steps = [(block, piece) for block in range(FEATURE_BLOCKS) for piece in range(PIECES)]
+    rows = [slice(block * P, (block + 1) * P) for block, piece in steps]
+    cols = [slice(piece * PIECE, (piece + 1) * PIECE) for block, piece in steps]
+
     with (
         tc.tile_pool(name="held", bufs=1) as held,
-        tc.tile_pool(name="work", bufs=2) as work,
+        tc.tile_pool(name="work", bufs=3) as work,
         tc.psum_pool(name="psum", bufs=8) as psum,
     ):
         offsets = held.tile([P, NODES // 16], U16, name="offsets")
         nc.sync.dma_start(offsets[:], offs)
         forget_weights = held.tile([P, FEATURES // P, FEATURES], BF16, name="forget_weights")
         nc.sync.dma_start(forget_weights[:], w_f.rearrange("(b p) c -> p b c", p=P))
-        hidden = [held.tile([P, HIDDEN_BLOCKS, PIECE], BF16, name=f"hidden{j}") for j in range(PIECES)]
-        nc.sync.dma_start(hidden[0][:], hidden_view[:, :, 0:PIECE])
+        hidden = [held.tile([P, HIDDEN_BLOCKS, PIECE], BF16, name=f"hidden{piece}") for piece in range(PIECES)]
+        forget_in = [held.tile([P, PIECE], F32, name=f"forget_in{t}") for t in range(len(steps))]
+        cells_in = [held.tile([P, CHILDREN, PIECE], F32, name=f"cells_in{t}") for t in range(len(steps))]
+        for t, (block, piece) in enumerate(steps):
+            if block == 0:
+                nc.sync.dma_start(hidden[piece][:], hidden_view[:, :, cols[t]])
+            nc.sync.dma_start(forget_in[t][:], f_input[rows[t], cols[t]])
+            nc.sync.dma_start(cells_in[t][:], cell_view[rows[t], :, cols[t]])
         gate_weights = held.tile([P, HIDDEN_BLOCKS, GATES * FEATURES], BF16, name="gate_weights")
         nc.sync.dma_start(gate_weights[:], w_iou.rearrange("(b p) m -> p b m", p=P))
+        gates_in = [held.tile([P, GATES, PIECE], F32, name=f"gates_in{t}") for t in range(len(steps))]
+        windows = [held.tile([P, STORE], F32, name=f"window{block}") for block in range(FEATURE_BLOCKS)]
+        for t, (block, piece) in enumerate(steps):
+            nc.sync.dma_start(gates_in[t][:], iou_view[rows[t], :, cols[t]])
+            if piece == 0:
+                nc.sync.dma_start(windows[block][:], base[rows[t], :])
 
-        windows, forget_in, gates_in, cells_in = [], {}, {}, {}
-        for block in range(FEATURE_BLOCKS):
-            rows = slice(block * P, (block + 1) * P)
-            for piece in range(PIECES):
-                cols = slice(piece * PIECE, (piece + 1) * PIECE)
-                step = (block, piece)
-                if block == 0 and piece > 0:
-                    nc.sync.dma_start(hidden[piece][:], hidden_view[:, :, cols])
-                forget_in[step] = held.tile([P, PIECE], F32, name=f"forget_in{block}{piece}")
-                nc.sync.dma_start(forget_in[step][:], f_input[rows, cols])
-                gates_in[step] = held.tile([P, GATES, PIECE], F32, name=f"gates_in{block}{piece}")
-                nc.sync.dma_start(gates_in[step][:], iou_view[rows, :, cols])
-                cells_in[step] = held.tile([P, CHILDREN, PIECE], F32, name=f"cells_in{block}{piece}")
-                nc.sync.dma_start(cells_in[step][:], cell_view[rows, :, cols])
-                if piece == 0:
-                    windows.append(held.tile([P, STORE], F32, name=f"window{block}"))
-                    nc.sync.dma_start(windows[block][:], base[rows, :])
-
-        for block in range(FEATURE_BLOCKS):
-            rows = slice(block * P, (block + 1) * P)
-            for piece in range(PIECES):
-                step = (block, piece)
-
-                forget = work.tile([P, CHILDREN, PIECE], F32, name="forget")
+        forget = []
+        kept = [held.tile([P, PIECE], F32, name=f"kept{t}") for t in range(len(steps))]
+        for t in range(len(steps) + 1):
+            if t < len(steps):
+                block, piece = steps[t]
+                forget.append(work.tile([P, CHILDREN, PIECE], F32, name="forget"))
                 for child in range(CHILDREN):
                     acc = psum.tile([P, PIECE], F32, name="acc")
                     for b in range(FEATURES // P):
                         nc.tensor.matmul(
                             acc[:],
-                            forget_weights[:, b, rows],
+                            forget_weights[:, b, rows[t]],
                             hidden[piece][:, child * (FEATURES // P) + b, :],
                             start=(b == 0),
                             stop=(b == FEATURES // P - 1),
                         )
-                    nc.vector.tensor_tensor(forget[:, child, :], acc[:], forget_in[step][:], ADD)
-                nc.scalar.activation(forget[:], forget[:], SIGMOID)
+                    nc.vector.tensor_tensor(forget[t][:, child, :], acc[:], forget_in[t][:], ADD)
+                nc.scalar.activation(forget[t][:], forget[t][:], SIGMOID)
+            if t > 0:
+                products = work.tile([P, CHILDREN, PIECE], F32, name="products")
+                nc.vector.tensor_tensor(products[:], forget[t - 1][:], cells_in[t - 1][:], MULT)
+                nc.vector.tensor_tensor(kept[t - 1][:], products[:, 0, :], products[:, 1, :], ADD)
 
-                gates = work.tile([P, GATES, PIECE], F32, name="gates")
-                for gate in range(GATES):
+        gates, cells = [], []
+        for t in range(len(steps) + 1):
+            if t > 0:
+                cells.append(work.tile([P, PIECE], F32, name="cell"))
+                cell = cells[t - 1]
+                nc.vector.tensor_tensor(cell[:], gates[t - 1][:, GATE_I, :], gates[t - 1][:, GATE_U, :], MULT)
+                nc.vector.tensor_tensor(cell[:], cell[:], kept[t - 1][:], ADD)
+                nc.scalar.activation(cell[:], cell[:], TANH)
+            if t < len(steps):
+                block, piece = steps[t]
+                gates.append(work.tile([P, GATES, PIECE], F32, name="gates"))
+                for gate in (GATE_I, GATE_U, GATE_O):
                     acc = psum.tile([P, PIECE], F32, name="acc")
                     for b in range(HIDDEN_BLOCKS):
                         nc.tensor.matmul(
@@ -87,22 +99,15 @@ def tile_generictreelstmcell_kernel(tc, base, child_h, child_c, f_input, iou_inp
                             start=(b == 0),
                             stop=(b == HIDDEN_BLOCKS - 1),
                         )
-                    nc.vector.scalar_tensor_tensor(gates[:, gate, :], gates_in[step][:, gate, :], 2.0, acc[:], MULT, ADD)
-                nc.scalar.activation(gates[:, GATE_I : GATE_O + 1, :], gates[:, GATE_I : GATE_O + 1, :], SIGMOID)
-                nc.scalar.activation(gates[:, GATE_U, :], gates[:, GATE_U, :], TANH)
-
-                kept = work.tile([P, CHILDREN, PIECE], F32, name="kept")
-                nc.vector.tensor_tensor(kept[:], forget[:], cells_in[step][:], MULT)
-                cell = work.tile([P, PIECE], F32, name="cell")
-                nc.vector.tensor_tensor(cell[:], gates[:, GATE_I, :], gates[:, GATE_U, :], MULT)
-                nc.vector.tensor_tensor(cell[:], cell[:], kept[:, 0, :], ADD)
-                nc.vector.tensor_tensor(cell[:], cell[:], kept[:, 1, :], ADD)
-                nc.scalar.activation(cell[:], cell[:], TANH)
-
+                    nc.vector.scalar_tensor_tensor(gates[t][:, gate, :], gates_in[t][:, gate, :], 2.0, acc[:], MULT, ADD)
+                    nc.scalar.activation(gates[t][:, gate, :], gates[t][:, gate, :], TANH if gate == GATE_U else SIGMOID)
+            if t > 0:
+                block, piece = steps[t - 1]
                 nc.vector.tensor_tensor(
                     windows[block][:].indirect(offsets[:, piece * (PIECE // 16) : (piece + 1) * (PIECE // 16)]),
-                    gates[:, GATE_O, :],
-                    cell[:],
+                    gates[t - 1][:, GATE_O, :],
+                    cells[t - 1][:],
                     MULT,
                 )
-            nc.sync.dma_start(out[rows, :], windows[block][:])
+                if piece == PIECES - 1:
+                    nc.sync.dma_start(out[rows[t - 1], :], windows[block][:])

@@ -19,6 +19,11 @@ GATE_I, GATE_O, GATE_U = 0, 1, 2
 FLOPS = 2 * NODES * (CHILDREN * FEATURES * FEATURES + CHILDREN * FEATURES * GATES * FEATURES)
 
 
+def accumulate(nc, acc, pairs):
+    for n, (weights, moving) in enumerate(pairs):
+        nc.tensor.matmul(acc, weights, moving, start=(n == 0), stop=(n == len(pairs) - 1))
+
+
 def tile_generictreelstmcell_kernel(tc, base, child_h, child_c, f_input, iou_input, w_f, w_iou, offs, out):
     nc = tc.nc
     hidden_view = child_h.rearrange("(b p) n -> p b n", p=P)
@@ -28,6 +33,7 @@ def tile_generictreelstmcell_kernel(tc, base, child_h, child_c, f_input, iou_inp
     steps = [(block, piece) for block in range(FEATURE_BLOCKS) for piece in range(PIECES)]
     rows = [slice(block * P, (block + 1) * P) for block, piece in steps]
     cols = [slice(piece * PIECE, (piece + 1) * PIECE) for block, piece in steps]
+    last = len(steps) - 1
 
     with (
         tc.tile_pool(name="held", bufs=1) as held,
@@ -38,6 +44,7 @@ def tile_generictreelstmcell_kernel(tc, base, child_h, child_c, f_input, iou_inp
         nc.sync.dma_start(offsets[:], offs)
         forget_weights = held.tile([P, FEATURES // P, FEATURES], BF16, name="forget_weights")
         nc.sync.dma_start(forget_weights[:], w_f.rearrange("(b p) c -> p b c", p=P))
+        gate_weights = held.tile([P, HIDDEN_BLOCKS, GATES * FEATURES], BF16, name="gate_weights")
         hidden = [held.tile([P, HIDDEN_BLOCKS, PIECE], BF16, name=f"hidden{piece}") for piece in range(PIECES)]
         forget_in = [held.tile([P, PIECE], F32, name=f"forget_in{t}") for t in range(len(steps))]
         cells_in = [held.tile([P, CHILDREN, PIECE], F32, name=f"cells_in{t}") for t in range(len(steps))]
@@ -46,68 +53,83 @@ def tile_generictreelstmcell_kernel(tc, base, child_h, child_c, f_input, iou_inp
                 nc.sync.dma_start(hidden[piece][:], hidden_view[:, :, cols[t]])
             nc.sync.dma_start(forget_in[t][:], f_input[rows[t], cols[t]])
             nc.sync.dma_start(cells_in[t][:], cell_view[rows[t], :, cols[t]])
-        gate_weights = held.tile([P, HIDDEN_BLOCKS, GATES * FEATURES], BF16, name="gate_weights")
         nc.sync.dma_start(gate_weights[:], w_iou.rearrange("(b p) m -> p b m", p=P))
         gates_in = [held.tile([P, GATES, PIECE], F32, name=f"gates_in{t}") for t in range(len(steps))]
         windows = [held.tile([P, STORE], F32, name=f"window{block}") for block in range(FEATURE_BLOCKS)]
         for t, (block, piece) in enumerate(steps):
             nc.sync.dma_start(gates_in[t][:], iou_view[rows[t], :, cols[t]])
-            if piece == 0:
+            if piece == 1:
                 nc.sync.dma_start(windows[block][:], base[rows[t], :])
 
-        forget = []
-        kept = [held.tile([P, PIECE], F32, name=f"kept{t}") for t in range(len(steps))]
-        for t in range(len(steps) + 1):
-            if t < len(steps):
-                block, piece = steps[t]
-                forget.append(work.tile([P, CHILDREN, PIECE], F32, name="forget"))
-                for child in range(CHILDREN):
-                    acc = psum.tile([P, PIECE], F32, name="acc")
-                    for b in range(FEATURES // P):
-                        nc.tensor.matmul(
-                            acc[:],
-                            forget_weights[:, b, rows[t]],
-                            hidden[piece][:, child * (FEATURES // P) + b, :],
-                            start=(b == 0),
-                            stop=(b == FEATURES // P - 1),
-                        )
-                    nc.vector.tensor_tensor(forget[t][:, child, :], acc[:], forget_in[t][:], ADD)
-                nc.scalar.activation(forget[t][:], forget[t][:], SIGMOID)
-            if t > 0:
-                products = work.tile([P, CHILDREN, PIECE], F32, name="products")
-                nc.vector.tensor_tensor(products[:], forget[t - 1][:], cells_in[t - 1][:], MULT)
-                nc.vector.tensor_tensor(kept[t - 1][:], products[:, 0, :], products[:, 1, :], ADD)
 
-        gates, cells = [], []
-        for t in range(len(steps) + 1):
-            if t > 0:
-                cells.append(work.tile([P, PIECE], F32, name="cell"))
-                cell = cells[t - 1]
-                nc.vector.tensor_tensor(cell[:], gates[t - 1][:, GATE_I, :], gates[t - 1][:, GATE_U, :], MULT)
-                nc.vector.tensor_tensor(cell[:], cell[:], kept[t - 1][:], ADD)
-                nc.scalar.activation(cell[:], cell[:], TANH)
-            if t < len(steps):
-                block, piece = steps[t]
-                gates.append(work.tile([P, GATES, PIECE], F32, name="gates"))
-                for gate in (GATE_I, GATE_U, GATE_O):
-                    acc = psum.tile([P, PIECE], F32, name="acc")
-                    for b in range(HIDDEN_BLOCKS):
-                        nc.tensor.matmul(
-                            acc[:],
-                            gate_weights[:, b, gate * FEATURES + block * P : gate * FEATURES + (block + 1) * P],
-                            hidden[piece][:, b, :],
-                            start=(b == 0),
-                            stop=(b == HIDDEN_BLOCKS - 1),
-                        )
-                    nc.vector.scalar_tensor_tensor(gates[t][:, gate, :], gates_in[t][:, gate, :], 2.0, acc[:], MULT, ADD)
-                    nc.scalar.activation(gates[t][:, gate, :], gates[t][:, gate, :], TANH if gate == GATE_U else SIGMOID)
-            if t > 0:
-                block, piece = steps[t - 1]
-                nc.vector.tensor_tensor(
-                    windows[block][:].indirect(offsets[:, piece * (PIECE // 16) : (piece + 1) * (PIECE // 16)]),
-                    gates[t - 1][:, GATE_O, :],
-                    cells[t - 1][:],
-                    MULT,
+        forget = [None] * len(steps)
+        kept = [held.tile([P, PIECE], F32, name=f"kept{t}") for t in range(len(steps))]
+
+        def forget_gates(t):
+            block, piece = steps[t]
+            forget[t] = work.tile([P, CHILDREN, PIECE], F32, name="forget")
+            for child in range(CHILDREN):
+                acc = psum.tile([P, PIECE], F32, name="acc")
+                accumulate(
+                    nc,
+                    acc[:],
+                    [
+                        (forget_weights[:, b, rows[t]], hidden[piece][:, child * (FEATURES // P) + b, :])
+                        for b in range(FEATURES // P)
+                    ],
                 )
-                if piece == PIECES - 1:
-                    nc.sync.dma_start(out[rows[t - 1], :], windows[block][:])
+                nc.vector.tensor_tensor(forget[t][:, child, :], acc[:], forget_in[t][:], ADD)
+            nc.scalar.activation(forget[t][:], forget[t][:], SIGMOID)
+
+        def keep(t):
+            nc.vector.tensor_tensor(forget[t][:], forget[t][:], cells_in[t][:], MULT)
+            nc.gpsimd.tensor_tensor(kept[t][:], forget[t][:, 0, :], forget[t][:, 1, :], ADD)
+
+        forget_gates(0)
+        for t in range(len(steps)):
+            if t < last:
+                forget_gates(t + 1)
+            keep(t)
+
+        gates = [None] * len(steps)
+        cells = [None] * len(steps)
+
+        def gate(t, which, function):
+            block, piece = steps[t]
+            columns = slice(which * FEATURES + block * P, which * FEATURES + (block + 1) * P)
+            acc = psum.tile([P, PIECE], F32, name="acc")
+            accumulate(nc, acc[:], [(gate_weights[:, b, columns], hidden[piece][:, b, :]) for b in range(HIDDEN_BLOCKS)])
+            nc.vector.scalar_tensor_tensor(gates[t][:, which, :], gates_in[t][:, which, :], 2.0, acc[:], MULT, ADD)
+            nc.scalar.activation(gates[t][:, which, :], gates[t][:, which, :], function)
+
+        def input_and_update(t):
+            gates[t] = work.tile([P, GATES, PIECE], F32, name="gates")
+            gate(t, GATE_I, SIGMOID)
+            gate(t, GATE_U, TANH)
+
+        def new_cell(t):
+            nc.vector.tensor_tensor(cells[t][:], cells[t][:], kept[t][:], ADD)
+            nc.scalar.activation(cells[t][:], cells[t][:], TANH)
+
+        def place(t):
+            block, piece = steps[t]
+            nc.vector.tensor_tensor(
+                windows[block][:].indirect(offsets[:, piece * (PIECE // 16) : (piece + 1) * (PIECE // 16)]),
+                gates[t][:, GATE_O, :],
+                cells[t][:],
+                MULT,
+            )
+            if piece == PIECES - 1:
+                nc.sync.dma_start(out[rows[t], :], windows[block][:])
+
+        input_and_update(0)
+        gate(0, GATE_O, SIGMOID)
+        for t in range(len(steps)):
+            cells[t] = work.tile([P, PIECE], F32, name="cell")
+            nc.gpsimd.tensor_tensor(cells[t][:], gates[t][:, GATE_I, :], gates[t][:, GATE_U, :], MULT)
+            if t < last:
+                input_and_update(t + 1)
+            new_cell(t)
+            if t < last:
+                gate(t + 1, GATE_O, SIGMOID)
+            place(t)

@@ -33,41 +33,55 @@ def tile_generictreelstmcell_kernel(tc, base, child_h, child_c, f_input, iou_inp
     steps = [(block, piece) for block in range(FEATURE_BLOCKS) for piece in range(PIECES)]
     rows = [slice(block * P, (block + 1) * P) for block, piece in steps]
     cols = [slice(piece * PIECE, (piece + 1) * PIECE) for block, piece in steps]
-    last = len(steps) - 1
 
     with (
         tc.tile_pool(name="held", bufs=1) as held,
-        tc.tile_pool(name="work", bufs=3) as work,
         tc.psum_pool(name="psum", bufs=8) as psum,
     ):
         offsets = held.tile([P, NODES // 16], U16, name="offsets")
-        nc.sync.dma_start(offsets[:], offs)
         forget_weights = held.tile([P, FEATURES // P, FEATURES], BF16, name="forget_weights")
-        nc.sync.dma_start(forget_weights[:], w_f.rearrange("(b p) c -> p b c", p=P))
         gate_weights = held.tile([P, HIDDEN_BLOCKS, GATES * FEATURES], BF16, name="gate_weights")
         hidden = [held.tile([P, HIDDEN_BLOCKS, PIECE], BF16, name=f"hidden{piece}") for piece in range(PIECES)]
+        windows = [held.tile([P, STORE], F32, name=f"window{block}") for block in range(FEATURE_BLOCKS)]
         forget_in = [held.tile([P, PIECE], F32, name=f"forget_in{t}") for t in range(len(steps))]
         cells_in = [held.tile([P, CHILDREN, PIECE], F32, name=f"cells_in{t}") for t in range(len(steps))]
-        for t, (block, piece) in enumerate(steps):
-            if block == 0:
-                nc.sync.dma_start(hidden[piece][:], hidden_view[:, :, cols[t]])
-            nc.sync.dma_start(forget_in[t][:], f_input[rows[t], cols[t]])
-            nc.sync.dma_start(cells_in[t][:], cell_view[rows[t], :, cols[t]])
-        nc.sync.dma_start(gate_weights[:], w_iou.rearrange("(b p) m -> p b m", p=P))
         gates_in = [held.tile([P, GATES, PIECE], F32, name=f"gates_in{t}") for t in range(len(steps))]
-        windows = [held.tile([P, STORE], F32, name=f"window{block}") for block in range(FEATURE_BLOCKS)]
-        for t, (block, piece) in enumerate(steps):
-            nc.sync.dma_start(gates_in[t][:], iou_view[rows[t], :, cols[t]])
-            if piece == 1:
-                nc.sync.dma_start(windows[block][:], base[rows[t], :])
-
-
-        forget = [None] * len(steps)
+        forget = [held.tile([P, CHILDREN, PIECE], F32, name=f"forget{t}") for t in range(len(steps))]
         kept = [held.tile([P, PIECE], F32, name=f"kept{t}") for t in range(len(steps))]
+        gates = [held.tile([P, GATES, PIECE], F32, name=f"gates{t}") for t in range(len(steps))]
+        cells = [held.tile([P, PIECE], F32, name=f"cell{t}") for t in range(len(steps))]
+        product = held.tile([P, PIECE], F32, name="product")
+
+        def load_forget_in(t):
+            nc.sync.dma_start(forget_in[t][:], f_input[rows[t], cols[t]])
+
+        def load_cells_in(t):
+            nc.sync.dma_start(cells_in[t][:], cell_view[rows[t], :, cols[t]])
+
+        def load_gates_in(t):
+            nc.sync.dma_start(gates_in[t][:], iou_view[rows[t], :, cols[t]])
+
+        nc.sync.dma_start(forget_weights[:], w_f.rearrange("(b p) c -> p b c", p=P))
+        for piece in range(PIECES):
+            nc.sync.dma_start(hidden[piece][:], hidden_view[:, :, cols[piece]])
+            load_forget_in(piece)
+        load_cells_in(0)
+        load_forget_in(2)
+        load_cells_in(1)
+        load_forget_in(3)
+        nc.sync.dma_start(gate_weights[:], w_iou.rearrange("(b p) m -> p b m", p=P))
+        load_cells_in(2)
+        load_gates_in(0)
+        load_cells_in(3)
+        load_gates_in(1)
+        load_gates_in(2)
+        nc.sync.dma_start(offsets[:], offs)
+        nc.sync.dma_start(windows[0][:], base[rows[0], :])
+        load_gates_in(3)
+        nc.sync.dma_start(windows[1][:], base[rows[2], :])
 
         def forget_gates(t):
             block, piece = steps[t]
-            forget[t] = work.tile([P, CHILDREN, PIECE], F32, name="forget")
             for child in range(CHILDREN):
                 acc = psum.tile([P, PIECE], F32, name="acc")
                 accumulate(
@@ -85,15 +99,6 @@ def tile_generictreelstmcell_kernel(tc, base, child_h, child_c, f_input, iou_inp
             nc.vector.tensor_tensor(forget[t][:], forget[t][:], cells_in[t][:], MULT)
             nc.gpsimd.tensor_tensor(kept[t][:], forget[t][:, 0, :], forget[t][:, 1, :], ADD)
 
-        forget_gates(0)
-        for t in range(len(steps)):
-            if t < last:
-                forget_gates(t + 1)
-            keep(t)
-
-        gates = [None] * len(steps)
-        cells = [None] * len(steps)
-
         def gate(t, which, function):
             block, piece = steps[t]
             columns = slice(which * FEATURES + block * P, which * FEATURES + (block + 1) * P)
@@ -103,12 +108,19 @@ def tile_generictreelstmcell_kernel(tc, base, child_h, child_c, f_input, iou_inp
             nc.scalar.activation(gates[t][:, which, :], gates[t][:, which, :], function)
 
         def input_and_update(t):
-            gates[t] = work.tile([P, GATES, PIECE], F32, name="gates")
             gate(t, GATE_I, SIGMOID)
             gate(t, GATE_U, TANH)
 
+        def output_gates(block):
+            for t in range(len(steps)):
+                if steps[t][0] == block:
+                    gate(t, GATE_O, SIGMOID)
+
+        def multiply(t):
+            nc.gpsimd.tensor_tensor(product[:], gates[t][:, GATE_I, :], gates[t][:, GATE_U, :], MULT)
+
         def new_cell(t):
-            nc.vector.tensor_tensor(cells[t][:], cells[t][:], kept[t][:], ADD)
+            nc.vector.tensor_tensor(cells[t][:], product[:], kept[t][:], ADD)
             nc.scalar.activation(cells[t][:], cells[t][:], TANH)
 
         def place(t):
@@ -122,14 +134,14 @@ def tile_generictreelstmcell_kernel(tc, base, child_h, child_c, f_input, iou_inp
             if piece == PIECES - 1:
                 nc.sync.dma_start(out[rows[t], :], windows[block][:])
 
-        input_and_update(0)
-        gate(0, GATE_O, SIGMOID)
-        for t in range(len(steps)):
-            cells[t] = work.tile([P, PIECE], F32, name="cell")
-            nc.gpsimd.tensor_tensor(cells[t][:], gates[t][:, GATE_I, :], gates[t][:, GATE_U, :], MULT)
-            if t < last:
-                input_and_update(t + 1)
-            new_cell(t)
-            if t < last:
-                gate(t + 1, GATE_O, SIGMOID)
-            place(t)
+        forget_gates(0)
+        forget_gates(1)
+        keep(0), forget_gates(2)
+        keep(1), forget_gates(3)
+        keep(2), input_and_update(0)
+        keep(3), input_and_update(1)
+        multiply(0), output_gates(0)
+        new_cell(0), multiply(1), input_and_update(2), place(0)
+        new_cell(1), multiply(2), input_and_update(3), place(1)
+        new_cell(2), multiply(3), output_gates(1)
+        new_cell(3), place(2), place(3)

@@ -50,7 +50,6 @@ def tile_generictreelstmcell_kernel(tc, base, child_h, child_c, f_input, iou_inp
         kept = [held.tile([P, PIECE], F32, name=f"kept{t}") for t in range(len(steps))]
         gates = [held.tile([P, GATES, PIECE], F32, name=f"gates{t}") for t in range(len(steps))]
         cells = [held.tile([P, PIECE], F32, name=f"cell{t}") for t in range(len(steps))]
-        product = held.tile([P, PIECE], F32, name="product")
 
         def load_forget_in(t):
             nc.sync.dma_start(forget_in[t][:], f_input[rows[t], cols[t]])
@@ -75,9 +74,9 @@ def tile_generictreelstmcell_kernel(tc, base, child_h, child_c, f_input, iou_inp
         load_cells_in(3)
         load_gates_in(1)
         load_gates_in(2)
+        load_gates_in(3)
         nc.sync.dma_start(offsets[:], offs)
         nc.sync.dma_start(windows[0][:], base[rows[0], :])
-        load_gates_in(3)
         nc.sync.dma_start(windows[1][:], base[rows[2], :])
 
         def forget_gates(t):
@@ -117,10 +116,10 @@ def tile_generictreelstmcell_kernel(tc, base, child_h, child_c, f_input, iou_inp
                     gate(t, GATE_O, SIGMOID)
 
         def multiply(t):
-            nc.gpsimd.tensor_tensor(product[:], gates[t][:, GATE_I, :], gates[t][:, GATE_U, :], MULT)
+            nc.gpsimd.tensor_tensor(cells[t][:], gates[t][:, GATE_I, :], gates[t][:, GATE_U, :], MULT)
 
         def new_cell(t):
-            nc.vector.tensor_tensor(cells[t][:], product[:], kept[t][:], ADD)
+            nc.vector.tensor_tensor(cells[t][:], cells[t][:], kept[t][:], ADD)
             nc.scalar.activation(cells[t][:], cells[t][:], TANH)
 
         def place(t):
@@ -141,7 +140,11 @@ def tile_generictreelstmcell_kernel(tc, base, child_h, child_c, f_input, iou_inp
         keep(2), input_and_update(0)
         keep(3), input_and_update(1)
         multiply(0), output_gates(0)
-        new_cell(0), multiply(1), input_and_update(2), place(0)
-        new_cell(1), multiply(2), input_and_update(3), place(1)
-        new_cell(2), multiply(3), output_gates(1)
-        new_cell(3), place(2), place(3)
+        multiply(1), input_and_update(2)
+        new_cell(0)
+        multiply(2), input_and_update(3)
+        new_cell(1), place(0)
+        multiply(3), output_gates(1)
+        new_cell(2), place(1)
+        new_cell(3), place(2)
+        place(3)

@@ -39,6 +39,7 @@ def tile_generictreelstmcell_kernel(tc, base, child_h, child_c, f_input, iou_inp
         tc.psum_pool(name="psum", bufs=8) as psum,
     ):
         offsets = held.tile([P, NODES // 16], U16, name="offsets")
+        twice = held.tile([P, P], F32, name="twice")
         forget_weights = held.tile([P, FEATURES // P, FEATURES], BF16, name="forget_weights")
         gate_weights = held.tile([P, HIDDEN_BLOCKS, GATES * FEATURES], BF16, name="gate_weights")
         hidden = [held.tile([P, HIDDEN_BLOCKS, PIECE], BF16, name=f"hidden{piece}") for piece in range(PIECES)]
@@ -61,23 +62,28 @@ def tile_generictreelstmcell_kernel(tc, base, child_h, child_c, f_input, iou_inp
             nc.sync.dma_start(gates_in[t][:], iou_view[rows[t], :, cols[t]])
 
         nc.sync.dma_start(forget_weights[:], w_f.rearrange("(b p) c -> p b c", p=P))
-        for piece in range(PIECES):
-            nc.sync.dma_start(hidden[piece][:], hidden_view[:, :, cols[piece]])
-            load_forget_in(piece)
+        nc.sync.dma_start(hidden[0][:], hidden_view[:, :, cols[0]])
+        load_forget_in(0)
+        nc.sync.dma_start(gate_weights[:], w_iou.rearrange("(b p) m -> p b m", p=P))
         load_cells_in(0)
+        load_gates_in(0)
+        nc.sync.dma_start(hidden[1][:], hidden_view[:, :, cols[1]])
+        load_forget_in(1)
         load_forget_in(2)
+        load_gates_in(1)
         load_cells_in(1)
         load_forget_in(3)
-        nc.sync.dma_start(gate_weights[:], w_iou.rearrange("(b p) m -> p b m", p=P))
-        load_cells_in(2)
-        load_gates_in(0)
-        load_cells_in(3)
-        load_gates_in(1)
-        load_gates_in(2)
-        load_gates_in(3)
         nc.sync.dma_start(offsets[:], offs)
         nc.sync.dma_start(windows[0][:], base[rows[0], :])
+        for t in (2, 3):
+            load_cells_in(t)
+            load_gates_in(t)
         nc.sync.dma_start(windows[1][:], base[rows[2], :])
+
+        nc.gpsimd.memset(twice[:], 0.0)
+        nc.gpsimd.affine_select(
+            out=twice[:], in_=twice[:], compare_op=mybir.AluOpType.not_equal, fill=2.0, base=0, pattern=[[-1, P]], channel_multiplier=1
+        )
 
         def forget_gates(t):
             block, piece = steps[t]
@@ -98,22 +104,30 @@ def tile_generictreelstmcell_kernel(tc, base, child_h, child_c, f_input, iou_inp
             nc.vector.tensor_tensor(forget[t][:], forget[t][:], cells_in[t][:], MULT)
             nc.gpsimd.tensor_tensor(kept[t][:], forget[t][:, 0, :], forget[t][:, 1, :], ADD)
 
-        def gate(t, which, function):
+        def gate_sum(t, which):
             block, piece = steps[t]
             columns = slice(which * FEATURES + block * P, which * FEATURES + (block + 1) * P)
+            return [(gate_weights[:, b, columns], hidden[piece][:, b, :]) for b in range(HIDDEN_BLOCKS)]
+
+        def tensor_adds(t, which):
+            return t == len(steps) - 1 or (t > 0 and which != GATE_O)
+
+        def gate(t, which, function):
             acc = psum.tile([P, PIECE], F32, name="acc")
-            accumulate(nc, acc[:], [(gate_weights[:, b, columns], hidden[piece][:, b, :]) for b in range(HIDDEN_BLOCKS)])
-            nc.vector.scalar_tensor_tensor(gates[t][:, which, :], gates_in[t][:, which, :], 2.0, acc[:], MULT, ADD)
-            nc.scalar.activation(gates[t][:, which, :], gates[t][:, which, :], function)
+            if tensor_adds(t, which):
+                accumulate(nc, acc[:], gate_sum(t, which) + [(twice[:], gates_in[t][:, which, :])])
+                nc.scalar.activation(gates[t][:, which, :], acc[:], function)
+            else:
+                accumulate(nc, acc[:], gate_sum(t, which))
+                nc.vector.scalar_tensor_tensor(gates[t][:, which, :], gates_in[t][:, which, :], 2.0, acc[:], MULT, ADD)
+                nc.scalar.activation(gates[t][:, which, :], gates[t][:, which, :], function)
 
         def input_and_update(t):
             gate(t, GATE_I, SIGMOID)
             gate(t, GATE_U, TANH)
 
-        def output_gates(block):
-            for t in range(len(steps)):
-                if steps[t][0] == block:
-                    gate(t, GATE_O, SIGMOID)
+        def output_gate(t):
+            gate(t, GATE_O, SIGMOID)
 
         def multiply(t):
             nc.gpsimd.tensor_tensor(cells[t][:], gates[t][:, GATE_I, :], gates[t][:, GATE_U, :], MULT)
@@ -133,18 +147,23 @@ def tile_generictreelstmcell_kernel(tc, base, child_h, child_c, f_input, iou_inp
             if piece == PIECES - 1:
                 nc.sync.dma_start(out[rows[t], :], windows[block][:])
 
+        def cell_gates(t):
+            input_and_update(t), multiply(t)
+
         forget_gates(0)
-        forget_gates(1)
-        keep(0), forget_gates(2)
-        keep(1), forget_gates(3)
-        keep(2), input_and_update(0)
-        keep(3), input_and_update(1)
-        multiply(0), output_gates(0)
-        multiply(1), input_and_update(2)
-        new_cell(0)
-        multiply(2), input_and_update(3)
-        new_cell(1), place(0)
-        multiply(3), output_gates(1)
-        new_cell(2), place(1)
-        new_cell(3), place(2)
-        place(3)
+        cell_gates(0)
+        keep(0), forget_gates(1)
+        output_gate(0)
+        keep(1), forget_gates(2)
+        cell_gates(1)
+        new_cell(0), place(0)
+        keep(2), forget_gates(3)
+        output_gate(1)
+        new_cell(1)
+        cell_gates(2)
+        keep(3), place(1)
+        output_gate(2)
+        new_cell(2)
+        cell_gates(3)
+        output_gate(3)
+        new_cell(3), place(2), place(3)

@@ -65,19 +65,20 @@ def tile_generictreelstmcell_kernel(tc, base, child_h, child_c, f_input, iou_inp
         nc.sync.dma_start(hidden[0][:], hidden_view[:, :, cols[0]])
         load_forget_in(0)
         nc.sync.dma_start(gate_weights[:], w_iou.rearrange("(b p) m -> p b m", p=P))
+        nc.sync.dma_start(hidden[1][:], hidden_view[:, :, cols[1]])
         load_cells_in(0)
         load_gates_in(0)
-        nc.sync.dma_start(hidden[1][:], hidden_view[:, :, cols[1]])
         load_forget_in(1)
         load_forget_in(2)
         load_gates_in(1)
-        load_cells_in(1)
-        load_forget_in(3)
         nc.sync.dma_start(offsets[:], offs)
         nc.sync.dma_start(windows[0][:], base[rows[0], :])
-        for t in (2, 3):
-            load_cells_in(t)
-            load_gates_in(t)
+        load_cells_in(1)
+        load_forget_in(3)
+        load_gates_in(2)
+        load_cells_in(2)
+        load_gates_in(3)
+        load_cells_in(3)
         nc.sync.dma_start(windows[1][:], base[rows[2], :])
 
         nc.gpsimd.memset(twice[:], 0.0)
@@ -102,19 +103,19 @@ def tile_generictreelstmcell_kernel(tc, base, child_h, child_c, f_input, iou_inp
 
         def keep(t):
             nc.vector.tensor_tensor(forget[t][:], forget[t][:], cells_in[t][:], MULT)
-            nc.gpsimd.tensor_tensor(kept[t][:], forget[t][:, 0, :], forget[t][:, 1, :], ADD)
+            nc.vector.tensor_tensor(kept[t][:], forget[t][:, 0, :], forget[t][:, 1, :], ADD)
 
         def gate_sum(t, which):
             block, piece = steps[t]
             columns = slice(which * FEATURES + block * P, which * FEATURES + (block + 1) * P)
             return [(gate_weights[:, b, columns], hidden[piece][:, b, :]) for b in range(HIDDEN_BLOCKS)]
 
-        def tensor_adds(t, which):
-            return t == len(steps) - 1 or (t > 0 and which != GATE_O)
+        def tensor_adds(t):
+            return t > 0
 
         def gate(t, which, function):
             acc = psum.tile([P, PIECE], F32, name="acc")
-            if tensor_adds(t, which):
+            if tensor_adds(t):
                 accumulate(nc, acc[:], gate_sum(t, which) + [(twice[:], gates_in[t][:, which, :])])
                 nc.scalar.activation(gates[t][:, which, :], acc[:], function)
             else:
@@ -154,16 +155,16 @@ def tile_generictreelstmcell_kernel(tc, base, child_h, child_c, f_input, iou_inp
         cell_gates(0)
         keep(0), forget_gates(1)
         output_gate(0)
-        keep(1), forget_gates(2)
+        new_cell(0), forget_gates(2)
         cell_gates(1)
-        new_cell(0), place(0)
-        keep(2), forget_gates(3)
+        place(0), keep(1), forget_gates(3)
         output_gate(1)
-        new_cell(1)
+        new_cell(1), keep(2)
         cell_gates(2)
-        keep(3), place(1)
-        output_gate(2)
-        new_cell(2)
+        place(1), keep(3)
         cell_gates(3)
+        new_cell(2)
+        output_gate(2)
+        new_cell(3)
         output_gate(3)
-        new_cell(3), place(2), place(3)
+        place(2), place(3)

@@ -77,9 +77,9 @@ def tile_generictreelstmcell_kernel(tc, base, child_h, child_c, f_input, iou_inp
         load_forget_in(3)
         load_gates_in(2)
         load_cells_in(2)
+        nc.sync.dma_start(windows[1][:], base[rows[2], :])
         load_gates_in(3)
         load_cells_in(3)
-        nc.sync.dma_start(windows[1][:], base[rows[2], :])
 
         nc.gpsimd.memset(twice[:], 0.0)
         nc.gpsimd.affine_select(

@@ -62,24 +62,22 @@ def tile_generictreelstmcell_kernel(tc, base, child_h, child_c, f_input, iou_inp
             nc.sync.dma_start(gates_in[t][:], iou_view[rows[t], :, cols[t]])
 
         nc.sync.dma_start(forget_weights[:], w_f.rearrange("(b p) c -> p b c", p=P))
-        nc.sync.dma_start(hidden[0][:], hidden_view[:, :, cols[0]])
-        load_forget_in(0)
+        for piece in range(PIECES):
+            nc.sync.dma_start(hidden[piece][:], hidden_view[:, :, cols[piece]])
+            load_forget_in(piece)
+            load_forget_in(PIECES + piece)
         nc.sync.dma_start(gate_weights[:], w_iou.rearrange("(b p) m -> p b m", p=P))
-        nc.sync.dma_start(hidden[1][:], hidden_view[:, :, cols[1]])
         load_cells_in(0)
         load_gates_in(0)
-        load_forget_in(1)
-        load_forget_in(2)
+        load_cells_in(1)
         load_gates_in(1)
         nc.sync.dma_start(offsets[:], offs)
         nc.sync.dma_start(windows[0][:], base[rows[0], :])
-        load_cells_in(1)
-        load_forget_in(3)
-        load_gates_in(2)
         load_cells_in(2)
+        load_gates_in(2)
         nc.sync.dma_start(windows[1][:], base[rows[2], :])
-        load_gates_in(3)
         load_cells_in(3)
+        load_gates_in(3)
 
         nc.gpsimd.memset(twice[:], 0.0)
         nc.gpsimd.affine_select(
@@ -111,7 +109,7 @@ def tile_generictreelstmcell_kernel(tc, base, child_h, child_c, f_input, iou_inp
             return [(gate_weights[:, b, columns], hidden[piece][:, b, :]) for b in range(HIDDEN_BLOCKS)]
 
         def tensor_adds(t):
-            return t > 0
+            return steps[t][0] > 0
 
         def gate(t, which, function):
             acc = psum.tile([P, PIECE], F32, name="acc")
@@ -151,19 +149,12 @@ def tile_generictreelstmcell_kernel(tc, base, child_h, child_c, f_input, iou_inp
         def cell_gates(t):
             input_and_update(t), multiply(t)
 
-        forget_gates(0)
-        cell_gates(0)
-        keep(0), forget_gates(1)
-        output_gate(0)
-        new_cell(0), forget_gates(2)
-        cell_gates(1)
-        place(0), keep(1), forget_gates(3)
-        output_gate(1)
-        new_cell(1), keep(2)
-        cell_gates(2)
-        place(1), keep(3)
-        cell_gates(3)
-        new_cell(2)
+        for t in (0, 2, 1, 3):
+            forget_gates(t)
+        keep(0), cell_gates(0), output_gate(0)
+        keep(1), new_cell(0), cell_gates(1), output_gate(1)
+        place(0), keep(2), new_cell(1), cell_gates(2)
+        place(1), new_cell(2), keep(3), cell_gates(3)
         output_gate(2)
         new_cell(3)
         output_gate(3)

@@ -10,10 +10,9 @@ TANH = mybir.ActivationFunctionType.Tanh
 
 P = 128
 FEATURES, CHILDREN, GATES, STORE, NODES = 256, 2, 3, 2048, 1024
-FEATURE_BLOCKS = FEATURES // P
-HIDDEN_BLOCKS = CHILDREN * FEATURES // P
+BLOCKS = FEATURES // P
 PIECE = 512
-PIECES = NODES // PIECE
+PIECES = [slice(start, start + PIECE) for start in range(0, NODES, PIECE)]
 GATE_I, GATE_O, GATE_U = 0, 1, 2
 
 FLOPS = 2 * NODES * (CHILDREN * FEATURES * FEATURES + CHILDREN * FEATURES * GATES * FEATURES)
@@ -26,136 +25,120 @@ def accumulate(nc, acc, pairs):
 
 def tile_generictreelstmcell_kernel(tc, base, child_h, child_c, f_input, iou_input, w_f, w_iou, offs, out):
     nc = tc.nc
-    hidden_view = child_h.rearrange("(b p) n -> p b n", p=P)
+    hidden_view = child_h.rearrange("(k b p) n -> k p b n", k=CHILDREN, p=P)
     cell_view = child_c.rearrange("(k c) n -> c k n", k=CHILDREN)
-    iou_view = iou_input.rearrange("(q c) n -> c q n", q=GATES)
-
-    steps = [(block, piece) for block in range(FEATURE_BLOCKS) for piece in range(PIECES)]
-    rows = [slice(block * P, (block + 1) * P) for block, piece in steps]
-    cols = [slice(piece * PIECE, (piece + 1) * PIECE) for block, piece in steps]
+    rows = [slice(block * P, (block + 1) * P) for block in range(BLOCKS)]
 
     with (
         tc.tile_pool(name="held", bufs=1) as held,
         tc.psum_pool(name="psum", bufs=8) as psum,
     ):
+        def held_by_block(name, *shape):
+            return [held.tile([P, *shape], F32, name=f"{name}{block}") for block in range(BLOCKS)]
+
         offsets = held.tile([P, NODES // 16], U16, name="offsets")
         twice = held.tile([P, P], F32, name="twice")
-        forget_weights = held.tile([P, FEATURES // P, FEATURES], BF16, name="forget_weights")
-        gate_weights = held.tile([P, HIDDEN_BLOCKS, GATES * FEATURES], BF16, name="gate_weights")
-        hidden = [held.tile([P, HIDDEN_BLOCKS, PIECE], BF16, name=f"hidden{piece}") for piece in range(PIECES)]
-        windows = [held.tile([P, STORE], F32, name=f"window{block}") for block in range(FEATURE_BLOCKS)]
-        forget_in = [held.tile([P, PIECE], F32, name=f"forget_in{t}") for t in range(len(steps))]
-        cells_in = [held.tile([P, CHILDREN, PIECE], F32, name=f"cells_in{t}") for t in range(len(steps))]
-        gates_in = [held.tile([P, GATES, PIECE], F32, name=f"gates_in{t}") for t in range(len(steps))]
-        forget = [held.tile([P, CHILDREN, PIECE], F32, name=f"forget{t}") for t in range(len(steps))]
-        kept = [held.tile([P, PIECE], F32, name=f"kept{t}") for t in range(len(steps))]
-        gates = [held.tile([P, GATES, PIECE], F32, name=f"gates{t}") for t in range(len(steps))]
-        cells = [held.tile([P, PIECE], F32, name=f"cell{t}") for t in range(len(steps))]
+        forget_weights = held.tile([P, BLOCKS, FEATURES], BF16, name="forget_weights")
+        gate_weights = held.tile([P, CHILDREN * BLOCKS, GATES * FEATURES], BF16, name="gate_weights")
+        hidden = [held.tile([P, BLOCKS, NODES], BF16, name=f"hidden{child}") for child in range(CHILDREN)]
+        windows = held_by_block("window", STORE)
+        forget_in = held_by_block("forget_in", NODES)
+        cells_in = held_by_block("cells_in", CHILDREN, NODES)
+        gates_in = held_by_block("gates_in", GATES, NODES)
+        forget = held_by_block("forget", CHILDREN, NODES)
+        kept = held_by_block("kept", NODES)
+        gates = held_by_block("gates", GATES, NODES)
+        cells = held_by_block("cell", NODES)
 
-        def load_forget_in(t):
-            nc.sync.dma_start(forget_in[t][:], f_input[rows[t], cols[t]])
-
-        def load_cells_in(t):
-            nc.sync.dma_start(cells_in[t][:], cell_view[rows[t], :, cols[t]])
-
-        def load_gates_in(t):
-            nc.sync.dma_start(gates_in[t][:], iou_view[rows[t], :, cols[t]])
+        def load_gate_in(block, which):
+            first = which * FEATURES + block * P
+            nc.sync.dma_start(gates_in[block][:, which, :], iou_input[first : first + P, :])
 
         nc.sync.dma_start(forget_weights[:], w_f.rearrange("(b p) c -> p b c", p=P))
-        for piece in range(PIECES):
-            nc.sync.dma_start(hidden[piece][:], hidden_view[:, :, cols[piece]])
-            load_forget_in(piece)
-            load_forget_in(PIECES + piece)
+        nc.sync.dma_start(hidden[0][:], hidden_view[0])
+        for block in range(BLOCKS):
+            nc.sync.dma_start(forget_in[block][:], f_input[rows[block], :])
+        nc.sync.dma_start(hidden[1][:], hidden_view[1])
         nc.sync.dma_start(gate_weights[:], w_iou.rearrange("(b p) m -> p b m", p=P))
-        load_cells_in(0)
-        load_gates_in(0)
-        load_cells_in(1)
-        load_gates_in(1)
+        nc.sync.dma_start(cells_in[0][:], cell_view[rows[0], :, :])
+        for which in (GATE_I, GATE_U, GATE_O):
+            load_gate_in(0, which)
+        nc.sync.dma_start(cells_in[1][:], cell_view[rows[1], :, :])
         nc.sync.dma_start(offsets[:], offs)
         nc.sync.dma_start(windows[0][:], base[rows[0], :])
-        load_cells_in(2)
-        load_gates_in(2)
-        nc.sync.dma_start(windows[1][:], base[rows[2], :])
-        load_cells_in(3)
-        load_gates_in(3)
+        for which in (GATE_I, GATE_U, GATE_O):
+            load_gate_in(1, which)
+        nc.sync.dma_start(windows[1][:], base[rows[1], :])
 
         nc.gpsimd.memset(twice[:], 0.0)
         nc.gpsimd.affine_select(
             out=twice[:], in_=twice[:], compare_op=mybir.AluOpType.not_equal, fill=2.0, base=0, pattern=[[-1, P]], channel_multiplier=1
         )
 
-        def forget_gates(t):
-            block, piece = steps[t]
-            for child in range(CHILDREN):
+        def forget_gate(block, child):
+            for nodes in PIECES:
                 acc = psum.tile([P, PIECE], F32, name="acc")
-                accumulate(
-                    nc,
-                    acc[:],
-                    [
-                        (forget_weights[:, b, rows[t]], hidden[piece][:, child * (FEATURES // P) + b, :])
-                        for b in range(FEATURES // P)
-                    ],
-                )
-                nc.vector.tensor_tensor(forget[t][:, child, :], acc[:], forget_in[t][:], ADD)
-            nc.scalar.activation(forget[t][:], forget[t][:], SIGMOID)
+                accumulate(nc, acc[:], [(forget_weights[:, b, rows[block]], hidden[child][:, b, nodes]) for b in range(BLOCKS)])
+                nc.vector.tensor_tensor(forget[block][:, child, nodes], acc[:], forget_in[block][:, nodes], ADD)
+            nc.scalar.activation(forget[block][:, child, :], forget[block][:, child, :], SIGMOID)
 
-        def keep(t):
-            nc.vector.tensor_tensor(forget[t][:], forget[t][:], cells_in[t][:], MULT)
-            nc.vector.tensor_tensor(kept[t][:], forget[t][:, 0, :], forget[t][:, 1, :], ADD)
+        def keep(block):
+            nc.vector.tensor_tensor(forget[block][:], forget[block][:], cells_in[block][:], MULT)
+            nc.vector.tensor_tensor(kept[block][:], forget[block][:, 0, :], forget[block][:, 1, :], ADD)
 
-        def gate_sum(t, which):
-            block, piece = steps[t]
+        def tensor_adds(block, which):
+            return block > 0 or which == GATE_O
+
+        def gate(block, which, function):
             columns = slice(which * FEATURES + block * P, which * FEATURES + (block + 1) * P)
-            return [(gate_weights[:, b, columns], hidden[piece][:, b, :]) for b in range(HIDDEN_BLOCKS)]
+            for nodes in PIECES:
+                acc = psum.tile([P, PIECE], F32, name="acc")
+                pairs = [
+                    (gate_weights[:, child * BLOCKS + b, columns], hidden[child][:, b, nodes])
+                    for child in range(CHILDREN)
+                    for b in range(BLOCKS)
+                ]
+                values, inputs = gates[block][:, which, nodes], gates_in[block][:, which, nodes]
+                if tensor_adds(block, which):
+                    accumulate(nc, acc[:], pairs + [(twice[:], inputs)])
+                    nc.scalar.activation(values, acc[:], function)
+                else:
+                    accumulate(nc, acc[:], pairs)
+                    nc.vector.scalar_tensor_tensor(values, inputs, 2.0, acc[:], MULT, ADD)
+                    nc.scalar.activation(values, values, function)
 
-        def tensor_adds(t):
-            return steps[t][0] > 0
+        def multiply(block):
+            nc.vector.tensor_tensor(cells[block][:], gates[block][:, GATE_I, :], gates[block][:, GATE_U, :], MULT)
 
-        def gate(t, which, function):
-            acc = psum.tile([P, PIECE], F32, name="acc")
-            if tensor_adds(t):
-                accumulate(nc, acc[:], gate_sum(t, which) + [(twice[:], gates_in[t][:, which, :])])
-                nc.scalar.activation(gates[t][:, which, :], acc[:], function)
-            else:
-                accumulate(nc, acc[:], gate_sum(t, which))
-                nc.vector.scalar_tensor_tensor(gates[t][:, which, :], gates_in[t][:, which, :], 2.0, acc[:], MULT, ADD)
-                nc.scalar.activation(gates[t][:, which, :], gates[t][:, which, :], function)
+        def new_cell(block):
+            for nodes in PIECES:
+                nc.vector.tensor_tensor(cells[block][:, nodes], cells[block][:, nodes], kept[block][:, nodes], ADD)
+                nc.scalar.activation(cells[block][:, nodes], cells[block][:, nodes], TANH)
 
-        def input_and_update(t):
-            gate(t, GATE_I, SIGMOID)
-            gate(t, GATE_U, TANH)
+        def place(block):
+            for nodes in PIECES:
+                nc.vector.tensor_tensor(
+                    windows[block][:].indirect(offsets[:, nodes.start // 16 : nodes.stop // 16]),
+                    gates[block][:, GATE_O, nodes],
+                    cells[block][:, nodes],
+                    MULT,
+                )
+            nc.sync.dma_start(out[rows[block], :], windows[block][:])
 
-        def output_gate(t):
-            gate(t, GATE_O, SIGMOID)
-
-        def multiply(t):
-            nc.gpsimd.tensor_tensor(cells[t][:], gates[t][:, GATE_I, :], gates[t][:, GATE_U, :], MULT)
-
-        def new_cell(t):
-            nc.vector.tensor_tensor(cells[t][:], cells[t][:], kept[t][:], ADD)
-            nc.scalar.activation(cells[t][:], cells[t][:], TANH)
-
-        def place(t):
-            block, piece = steps[t]
-            nc.vector.tensor_tensor(
-                windows[block][:].indirect(offsets[:, piece * (PIECE // 16) : (piece + 1) * (PIECE // 16)]),
-                gates[t][:, GATE_O, :],
-                cells[t][:],
-                MULT,
-            )
-            if piece == PIECES - 1:
-                nc.sync.dma_start(out[rows[t], :], windows[block][:])
-
-        def cell_gates(t):
-            input_and_update(t), multiply(t)
-
-        for t in (0, 2, 1, 3):
-            forget_gates(t)
-        keep(0), cell_gates(0), output_gate(0)
-        keep(1), new_cell(0), cell_gates(1), output_gate(1)
-        place(0), keep(2), new_cell(1), cell_gates(2)
-        place(1), new_cell(2), keep(3), cell_gates(3)
-        output_gate(2)
-        new_cell(3)
-        output_gate(3)
-        place(2), place(3)
+        for child in range(CHILDREN):
+            for block in range(BLOCKS):
+                forget_gate(block, child)
+        keep(0)
+        gate(0, GATE_I, SIGMOID)
+        gate(0, GATE_U, TANH)
+        multiply(0)
+        gate(0, GATE_O, SIGMOID)
+        keep(1)
+        new_cell(0)
+        gate(1, GATE_I, SIGMOID)
+        gate(1, GATE_U, TANH)
+        place(0)
+        gate(1, GATE_O, SIGMOID)
+        multiply(1)
+        new_cell(1)
+        place(1)

@@ -61,9 +61,10 @@ def tile_generictreelstmcell_kernel(tc, base, child_h, child_c, f_input, iou_inp
         nc.sync.dma_start(hidden[1][:], hidden_view[1])
         nc.sync.dma_start(gate_weights[:], w_iou.rearrange("(b p) m -> p b m", p=P))
         nc.sync.dma_start(cells_in[0][:], cell_view[rows[0], :, :])
-        for which in (GATE_I, GATE_U, GATE_O):
-            load_gate_in(0, which)
+        load_gate_in(0, GATE_I)
+        load_gate_in(0, GATE_U)
         nc.sync.dma_start(cells_in[1][:], cell_view[rows[1], :, :])
+        load_gate_in(0, GATE_O)
         nc.sync.dma_start(offsets[:], offs)
         nc.sync.dma_start(windows[0][:], base[rows[0], :])
         for which in (GATE_I, GATE_U, GATE_O):
@@ -82,9 +83,9 @@ def tile_generictreelstmcell_kernel(tc, base, child_h, child_c, f_input, iou_inp
                 nc.vector.tensor_tensor(forget[block][:, child, nodes], acc[:], forget_in[block][:, nodes], ADD)
             nc.scalar.activation(forget[block][:, child, :], forget[block][:, child, :], SIGMOID)
 
-        def keep(block):
+        def keep(block, adder):
             nc.vector.tensor_tensor(forget[block][:], forget[block][:], cells_in[block][:], MULT)
-            nc.vector.tensor_tensor(kept[block][:], forget[block][:, 0, :], forget[block][:, 1, :], ADD)
+            adder.tensor_tensor(kept[block][:], forget[block][:, 0, :], forget[block][:, 1, :], ADD)
 
         def tensor_adds(block, which):
             return block > 0 or which == GATE_O
@@ -107,13 +108,12 @@ def tile_generictreelstmcell_kernel(tc, base, child_h, child_c, f_input, iou_inp
                     nc.vector.scalar_tensor_tensor(values, inputs, 2.0, acc[:], MULT, ADD)
                     nc.scalar.activation(values, values, function)
 
-        def multiply(block):
-            nc.vector.tensor_tensor(cells[block][:], gates[block][:, GATE_I, :], gates[block][:, GATE_U, :], MULT)
-
         def new_cell(block):
             for nodes in PIECES:
-                nc.vector.tensor_tensor(cells[block][:, nodes], cells[block][:, nodes], kept[block][:, nodes], ADD)
-                nc.scalar.activation(cells[block][:, nodes], cells[block][:, nodes], TANH)
+                cell = cells[block][:, nodes]
+                nc.vector.tensor_tensor(cell, gates[block][:, GATE_I, nodes], gates[block][:, GATE_U, nodes], MULT)
+                nc.vector.tensor_tensor(cell, cell, kept[block][:, nodes], ADD)
+                nc.scalar.activation(cell, cell, TANH)
 
         def place(block):
             for nodes in PIECES:
@@ -128,17 +128,15 @@ def tile_generictreelstmcell_kernel(tc, base, child_h, child_c, f_input, iou_inp
         for child in range(CHILDREN):
             for block in range(BLOCKS):
                 forget_gate(block, child)
-        keep(0)
+        keep(0, nc.gpsimd)
         gate(0, GATE_I, SIGMOID)
         gate(0, GATE_U, TANH)
-        multiply(0)
         gate(0, GATE_O, SIGMOID)
-        keep(1)
         new_cell(0)
+        keep(1, nc.vector)
         gate(1, GATE_I, SIGMOID)
         gate(1, GATE_U, TANH)
         place(0)
         gate(1, GATE_O, SIGMOID)
-        multiply(1)
         new_cell(1)
         place(1)

@@ -54,17 +54,23 @@ def tile_generictreelstmcell_kernel(tc, base, child_h, child_c, f_input, iou_inp
             first = which * FEATURES + block * P
             nc.sync.dma_start(gates_in[block][:, which, :], iou_input[first : first + P, :])
 
+        def load_gate_weights(which):
+            columns = slice(which * FEATURES, (which + 1) * FEATURES)
+            nc.sync.dma_start(gate_weights[:, :, columns], w_iou.rearrange("(b p) m -> p b m", p=P)[:, :, columns])
+
         nc.sync.dma_start(forget_weights[:], w_f.rearrange("(b p) c -> p b c", p=P))
         nc.sync.dma_start(hidden[0][:], hidden_view[0])
-        for block in range(BLOCKS):
-            nc.sync.dma_start(forget_in[block][:], f_input[rows[block], :])
+        nc.sync.dma_start(forget_in[0][:], f_input[rows[0], :])
         nc.sync.dma_start(hidden[1][:], hidden_view[1])
-        nc.sync.dma_start(gate_weights[:], w_iou.rearrange("(b p) m -> p b m", p=P))
+        nc.sync.dma_start(forget_in[1][:], f_input[rows[1], :])
+        load_gate_weights(GATE_I)
         nc.sync.dma_start(cells_in[0][:], cell_view[rows[0], :, :])
+        load_gate_weights(GATE_U)
         load_gate_in(0, GATE_I)
         load_gate_in(0, GATE_U)
-        nc.sync.dma_start(cells_in[1][:], cell_view[rows[1], :, :])
+        load_gate_weights(GATE_O)
         load_gate_in(0, GATE_O)
+        nc.sync.dma_start(cells_in[1][:], cell_view[rows[1], :, :])
         nc.sync.dma_start(offsets[:], offs)
         nc.sync.dma_start(windows[0][:], base[rows[0], :])
         for which in (GATE_I, GATE_U, GATE_O):
@@ -109,14 +115,15 @@ def tile_generictreelstmcell_kernel(tc, base, child_h, child_c, f_input, iou_inp
                     nc.scalar.activation(values, values, function)
 
         def new_cell(block):
-            for nodes in PIECES:
-                cell = cells[block][:, nodes]
+            pieces = [cells[block][:, nodes] for nodes in PIECES]
+            for cell, nodes in zip(pieces, PIECES):
                 nc.vector.tensor_tensor(cell, gates[block][:, GATE_I, nodes], gates[block][:, GATE_U, nodes], MULT)
+            for cell, nodes in zip(pieces, PIECES):
                 nc.vector.tensor_tensor(cell, cell, kept[block][:, nodes], ADD)
                 nc.scalar.activation(cell, cell, TANH)
 
-        def place(block):
-            for nodes in PIECES:
+        def place(block, runs):
+            for nodes in runs:
                 nc.vector.tensor_tensor(
                     windows[block][:].indirect(offsets[:, nodes.start // 16 : nodes.stop // 16]),
                     gates[block][:, GATE_O, nodes],
@@ -125,8 +132,8 @@ def tile_generictreelstmcell_kernel(tc, base, child_h, child_c, f_input, iou_inp
                 )
             nc.sync.dma_start(out[rows[block], :], windows[block][:])
 
-        for child in range(CHILDREN):
-            for block in range(BLOCKS):
+        for block in range(BLOCKS):
+            for child in range(CHILDREN):
                 forget_gate(block, child)
         keep(0, nc.gpsimd)
         gate(0, GATE_I, SIGMOID)
@@ -136,7 +143,7 @@ def tile_generictreelstmcell_kernel(tc, base, child_h, child_c, f_input, iou_inp
         keep(1, nc.vector)
         gate(1, GATE_I, SIGMOID)
         gate(1, GATE_U, TANH)
-        place(0)
+        place(0, [slice(0, NODES)])
         gate(1, GATE_O, SIGMOID)
         new_cell(1)
-        place(1)
+        place(1, PIECES)

@@ -54,8 +54,8 @@ def tile_generictreelstmcell_kernel(tc, base, child_h, child_c, f_input, iou_inp
             first = which * FEATURES + block * P
             nc.sync.dma_start(gates_in[block][:, which, :], iou_input[first : first + P, :])
 
-        def load_gate_weights(which):
-            columns = slice(which * FEATURES, (which + 1) * FEATURES)
+        def load_gate_weights(first, last):
+            columns = slice(first * FEATURES, (last + 1) * FEATURES)
             nc.sync.dma_start(gate_weights[:, :, columns], w_iou.rearrange("(b p) m -> p b m", p=P)[:, :, columns])
 
         nc.sync.dma_start(forget_weights[:], w_f.rearrange("(b p) c -> p b c", p=P))
@@ -63,12 +63,11 @@ def tile_generictreelstmcell_kernel(tc, base, child_h, child_c, f_input, iou_inp
         nc.sync.dma_start(forget_in[0][:], f_input[rows[0], :])
         nc.sync.dma_start(hidden[1][:], hidden_view[1])
         nc.sync.dma_start(forget_in[1][:], f_input[rows[1], :])
-        load_gate_weights(GATE_I)
+        load_gate_weights(GATE_I, GATE_I)
         nc.sync.dma_start(cells_in[0][:], cell_view[rows[0], :, :])
-        load_gate_weights(GATE_U)
+        load_gate_weights(GATE_O, GATE_U)
         load_gate_in(0, GATE_I)
         load_gate_in(0, GATE_U)
-        load_gate_weights(GATE_O)
         load_gate_in(0, GATE_O)
         nc.sync.dma_start(cells_in[1][:], cell_view[rows[1], :, :])
         nc.sync.dma_start(offsets[:], offs)

import concourse.mybir as mybir

F32 = mybir.dt.float32
BF16 = mybir.dt.bfloat16
U16 = mybir.dt.uint16
ADD = mybir.AluOpType.add
MULT = mybir.AluOpType.mult
SIGMOID = mybir.ActivationFunctionType.Sigmoid
TANH = mybir.ActivationFunctionType.Tanh

P = 128
FEATURES, CHILDREN, GATES, STORE, NODES = 256, 2, 3, 2048, 1024
BLOCKS = FEATURES // P
PIECE = 512
PIECES = [slice(start, start + PIECE) for start in range(0, NODES, PIECE)]
GATE_I, GATE_O, GATE_U = 0, 1, 2

FLOPS = 2 * NODES * (CHILDREN * FEATURES * FEATURES + CHILDREN * FEATURES * GATES * FEATURES)


def accumulate(nc, acc, pairs):
    for n, (weights, moving) in enumerate(pairs):
        nc.tensor.matmul(acc, weights, moving, start=(n == 0), stop=(n == len(pairs) - 1))


def tile_generictreelstmcell_kernel(tc, base, child_h, child_c, f_input, iou_input, w_f, w_iou, offs, out):
    nc = tc.nc
    hidden_view = child_h.rearrange("(k b p) n -> k p b n", k=CHILDREN, p=P)
    cell_view = child_c.rearrange("(k c) n -> c k n", k=CHILDREN)
    rows = [slice(block * P, (block + 1) * P) for block in range(BLOCKS)]

    with (
        tc.tile_pool(name="held", bufs=1) as held,
        tc.psum_pool(name="psum", bufs=8) as psum,
    ):
        def held_by_block(name, *shape):
            return [held.tile([P, *shape], F32, name=f"{name}{block}") for block in range(BLOCKS)]

        offsets = held.tile([P, NODES // 16], U16, name="offsets")
        twice = held.tile([P, P], F32, name="twice")
        forget_weights = held.tile([P, BLOCKS, FEATURES], BF16, name="forget_weights")
        gate_weights = held.tile([P, CHILDREN * BLOCKS, GATES * FEATURES], BF16, name="gate_weights")
        hidden = [held.tile([P, BLOCKS, NODES], BF16, name=f"hidden{child}") for child in range(CHILDREN)]
        windows = held_by_block("window", STORE)
        forget_in = held_by_block("forget_in", NODES)
        cells_in = held_by_block("cells_in", CHILDREN, NODES)
        gates_in = held_by_block("gates_in", GATES, NODES)
        forget = held_by_block("forget", CHILDREN, NODES)
        kept = held_by_block("kept", NODES)
        gates = held_by_block("gates", GATES, NODES)
        cells = held_by_block("cell", NODES)

        def load_gate_in(block, which):
            first = which * FEATURES + block * P
            nc.sync.dma_start(gates_in[block][:, which, :], iou_input[first : first + P, :])

        def load_gate_weights(first, last):
            columns = slice(first * FEATURES, (last + 1) * FEATURES)
            nc.sync.dma_start(gate_weights[:, :, columns], w_iou.rearrange("(b p) m -> p b m", p=P)[:, :, columns])

        nc.sync.dma_start(forget_weights[:], w_f.rearrange("(b p) c -> p b c", p=P))
        nc.sync.dma_start(hidden[0][:], hidden_view[0])
        nc.sync.dma_start(forget_in[0][:], f_input[rows[0], :])
        nc.sync.dma_start(hidden[1][:], hidden_view[1])
        nc.sync.dma_start(forget_in[1][:], f_input[rows[1], :])
        load_gate_weights(GATE_I, GATE_I)
        nc.sync.dma_start(cells_in[0][:], cell_view[rows[0], :, :])
        load_gate_weights(GATE_O, GATE_U)
        load_gate_in(0, GATE_I)
        load_gate_in(0, GATE_U)
        load_gate_in(0, GATE_O)
        nc.sync.dma_start(cells_in[1][:], cell_view[rows[1], :, :])
        nc.sync.dma_start(offsets[:], offs)
        nc.sync.dma_start(windows[0][:], base[rows[0], :])
        for which in (GATE_I, GATE_U, GATE_O):
            load_gate_in(1, which)
        nc.sync.dma_start(windows[1][:], base[rows[1], :])

        nc.gpsimd.memset(twice[:], 0.0)
        nc.gpsimd.affine_select(
            out=twice[:], in_=twice[:], compare_op=mybir.AluOpType.not_equal, fill=2.0, base=0, pattern=[[-1, P]], channel_multiplier=1
        )

        def forget_gate(block, child):
            for nodes in PIECES:
                acc = psum.tile([P, PIECE], F32, name="acc")
                accumulate(nc, acc[:], [(forget_weights[:, b, rows[block]], hidden[child][:, b, nodes]) for b in range(BLOCKS)])
                nc.vector.tensor_tensor(forget[block][:, child, nodes], acc[:], forget_in[block][:, nodes], ADD)
            nc.scalar.activation(forget[block][:, child, :], forget[block][:, child, :], SIGMOID)

        def keep(block, adder):
            nc.vector.tensor_tensor(forget[block][:], forget[block][:], cells_in[block][:], MULT)
            adder.tensor_tensor(kept[block][:], forget[block][:, 0, :], forget[block][:, 1, :], ADD)

        def tensor_adds(block, which):
            return block > 0 or which == GATE_O

        def gate(block, which, function):
            columns = slice(which * FEATURES + block * P, which * FEATURES + (block + 1) * P)
            for nodes in PIECES:
                acc = psum.tile([P, PIECE], F32, name="acc")
                pairs = [
                    (gate_weights[:, child * BLOCKS + b, columns], hidden[child][:, b, nodes])
                    for child in range(CHILDREN)
                    for b in range(BLOCKS)
                ]
                values, inputs = gates[block][:, which, nodes], gates_in[block][:, which, nodes]
                if tensor_adds(block, which):
                    accumulate(nc, acc[:], pairs + [(twice[:], inputs)])
                    nc.scalar.activation(values, acc[:], function)
                else:
                    accumulate(nc, acc[:], pairs)
                    nc.vector.scalar_tensor_tensor(values, inputs, 2.0, acc[:], MULT, ADD)
                    nc.scalar.activation(values, values, function)

        def new_cell(block):
            pieces = [cells[block][:, nodes] for nodes in PIECES]
            for cell, nodes in zip(pieces, PIECES):
                nc.vector.tensor_tensor(cell, gates[block][:, GATE_I, nodes], gates[block][:, GATE_U, nodes], MULT)
            for cell, nodes in zip(pieces, PIECES):
                nc.vector.tensor_tensor(cell, cell, kept[block][:, nodes], ADD)
                nc.scalar.activation(cell, cell, TANH)

        def place(block, runs):
            for nodes in runs:
                nc.vector.tensor_tensor(
                    windows[block][:].indirect(offsets[:, nodes.start // 16 : nodes.stop // 16]),
                    gates[block][:, GATE_O, nodes],
                    cells[block][:, nodes],
                    MULT,
                )
            nc.sync.dma_start(out[rows[block], :], windows[block][:])

        for block in range(BLOCKS):
            for child in range(CHILDREN):
                forget_gate(block, child)
        keep(0, nc.gpsimd)
        gate(0, GATE_I, SIGMOID)
        gate(0, GATE_U, TANH)
        gate(0, GATE_O, SIGMOID)
        new_cell(0)
        keep(1, nc.vector)
        gate(1, GATE_I, SIGMOID)
        gate(1, GATE_U, TANH)
        place(0, [slice(0, NODES)])
        gate(1, GATE_O, SIGMOID)
        new_cell(1)
        place(1, PIECES)
